import numpy as np
import ml_dtypes


def mxq(x, axis, fmt="e4m3"):
    dtype, down = {"e4m3": (ml_dtypes.float8_e4m3fn, 7), "e5m2": (ml_dtypes.float8_e5m2, 14)}[fmt]
    v = np.moveaxis(np.asarray(x, np.float32).astype(ml_dtypes.bfloat16).astype(np.float64), axis, -1)
    blocks = v.reshape(v.shape[:-1] + (-1, 32))
    amax = np.abs(blocks).max(-1, keepdims=True)
    byte = np.maximum(np.where(amax > 0, np.frexp(amax)[1] - 1 + 127, 0) - down, 1)
    scale = np.exp2(byte - 127.0)
    codes = (blocks / scale).astype(np.float32).astype(dtype).astype(np.float64)
    return np.moveaxis((codes * scale).reshape(v.shape), -1, axis)


WIDE = False


def mx_kscale(k):
    if not WIDE:
        return np.ones(k)
    levels = np.array([10, -10, 5, -5, 0])
    a = np.random.permutation(np.resize(levels, k // 512 * 4)).reshape(k // 512, 4)
    idx = np.arange(k)
    return np.exp2(a[idx // 512, idx % 128 // 32])


BF16 = ml_dtypes.bfloat16


def bf(x):
    return np.asarray(x, np.float32).astype(BF16)


def f64(x):
    return np.asarray(x).astype(np.float64)


E2M1 = np.array([0.0, 0.5, 1.0, 1.5, 2.0, 3.0, 4.0, 6.0, -0.0, -0.5, -1.0, -1.5, -2.0, -3.0, -4.0, -6.0])


def pack_weight(w, fmt):
    k, n = w.shape
    w = f64(bf(w)).reshape(k // 32, 32, n)
    amax = np.abs(w).max(1)
    if fmt == "e4m3":
        byte = np.frexp(amax)[1] - 1 + 127 - 7
    else:
        mant, ex = np.frexp(amax / 6.0)
        byte = np.where(mant > 0.5, ex, ex - 1) + 127
    byte = np.clip(np.where(amax > 0, byte, 1), 1, 254)
    scaled = (w * np.exp2(127.0 - byte)[:, None, :]).reshape(k, n).astype(np.float32)
    by_word = np.ascontiguousarray(scaled.reshape(k // 512, 128, 4, n).transpose(0, 1, 3, 2))
    if fmt == "e4m3":
        words = by_word.astype(ml_dtypes.float8_e4m3fn).view(np.uint8)
    else:
        c = by_word.astype(ml_dtypes.float4_e2m1fn).view(np.uint8) & 0xF
        words = c[..., 0::2] | (c[..., 1::2] << 4)
    return np.ascontiguousarray(words), np.ascontiguousarray(byte.astype(np.uint8).reshape(k // 512, 16, n))


def unpack_weight(words, scales, fmt):
    g, p, n, _ = words.shape
    if fmt == "e4m3":
        vals = np.ascontiguousarray(words).view(ml_dtypes.float8_e4m3fn).astype(np.float64)
    else:
        nib = np.empty((g, p, n, 4), np.uint8)
        nib[..., 0::2] = words & 0xF
        nib[..., 1::2] = words >> 4
        vals = E2M1[nib]
    vals = vals * np.repeat(np.exp2(scales.astype(np.float64) - 127.0), 8, axis=1)[..., None]
    return vals.transpose(0, 1, 3, 2).reshape(g * 512, n)


B, DIN, F, NCLS, NV = 4096, 1024, 128, 18, 3
S_NM = 2.0 / np.sqrt(DIN)
S_AN = 0.25 * np.sqrt(F / DIN)
FMT = "e4m3"


def draw_view():
    s = mx_kscale(DIN)
    x = bf(np.random.standard_normal((B, DIN)) * s)
    nm_words, nm_scales = pack_weight(np.random.standard_normal((DIN, F)) * S_NM / s[:, None], FMT)
    an_words, an_scales = pack_weight(np.random.standard_normal((DIN, F)) * S_AN / s[:, None], FMT)
    return x, nm_words, nm_scales, an_words, an_scales


def setup_inputs():
    x_dash, Wd_nm_words, Wd_nm_scales, Wd_an_words, Wd_an_scales = draw_view()
    x_rear, Wr_nm_words, Wr_nm_scales, Wr_an_words, Wr_an_scales = draw_view()
    x_right, Wt_nm_words, Wt_nm_scales, Wt_an_words, Wt_an_scales = draw_view()
    return {"x_dash": x_dash, "x_rear": x_rear, "x_right": x_right,
            "Wd_nm_words": Wd_nm_words, "Wd_nm_scales": Wd_nm_scales,
            "Wd_an_words": Wd_an_words, "Wd_an_scales": Wd_an_scales,
            "Wr_nm_words": Wr_nm_words, "Wr_nm_scales": Wr_nm_scales,
            "Wr_an_words": Wr_an_words, "Wr_an_scales": Wr_an_scales,
            "Wt_nm_words": Wt_nm_words, "Wt_nm_scales": Wt_nm_scales,
            "Wt_an_words": Wt_an_words, "Wt_an_scales": Wt_an_scales}


def branch(x, nm_words, nm_scales, an_words, an_scales):
    xq = mxq(f64(x), 1, "e4m3")
    nm = xq @ unpack_weight(nm_words, nm_scales, FMT)
    an = xq @ unpack_weight(an_words, an_scales, FMT)
    return np.mean(an, axis=1, keepdims=True) * nm


def reference(x_dash, x_rear, x_right, Wd_nm_words, Wd_nm_scales, Wd_an_words, Wd_an_scales, Wr_nm_words, Wr_nm_scales, Wr_an_words, Wr_an_scales, Wt_nm_words, Wt_nm_scales, Wt_an_words, Wt_an_scales):
    v = np.concatenate([branch(x_dash, Wd_nm_words, Wd_nm_scales, Wd_an_words, Wd_an_scales), branch(x_rear, Wr_nm_words, Wr_nm_scales, Wr_an_words, Wr_an_scales), branch(x_right, Wt_nm_words, Wt_nm_scales, Wt_an_words, Wt_an_scales)], axis=1)
    return v.reshape(v.shape[0], F, NV).mean(axis=-1)

@@ -1,0 +1,176 @@
+from contextlib import ExitStack
+
+import concourse.mybir as mybir
+from concourse.masks import make_identity
+
+F32 = mybir.dt.float32
+BF16 = mybir.dt.bfloat16
+I32 = mybir.dt.int32
+U32 = mybir.dt.uint32
+U8 = mybir.dt.uint8
+FP8X4 = mybir.dt.float8_e4m3fn_x4
+ADD = mybir.AluOpType.add
+MULT = mybir.AluOpType.mult
+X_AXIS = mybir.AxisListType.X
+
+P = 128
+PACK = 4
+K_PASS = P * PACK
+B, DIN, F, VIEWS = 4096, 1024, 128, 3
+PASSES = DIN // K_PASS
+PAIRS = PACK // 2
+PASS_WORDS = K_PASS // 2
+TILES = 4
+CHUNKS = B // (P * TILES)
+ROUNDS = CHUNKS * VIEWS
+BANK_TILES = 2
+AHEAD = 4
+QUADRANTS = 4
+
+FLOPS = 2 * 2 * VIEWS * B * DIN * F
+
+
+def tile_fusion_r3d_pa_t_kernel(
+    tc,
+    x_dash, x_rear, x_right,
+    Wd_nm_words, Wd_nm_scales, Wd_an_words, Wd_an_scales,
+    Wr_nm_words, Wr_nm_scales, Wr_an_words, Wr_an_scales,
+    Wt_nm_words, Wt_nm_scales, Wt_an_words, Wt_an_scales,
+    out,
+):
+    nc = tc.nc
+    x_chunks = [
+        x.rearrange("(c p j) k -> c p j k", p=P, j=TILES) for x in (x_dash, x_rear, x_right)
+    ]
+    out_chunks = out.rearrange("(c p j) n -> c p j n", p=P, j=TILES)
+    weights = [
+        ((Wd_nm_words, Wd_nm_scales), (Wd_an_words, Wd_an_scales)),
+        ((Wr_nm_words, Wr_nm_scales), (Wr_an_words, Wr_an_scales)),
+        ((Wt_nm_words, Wt_nm_scales), (Wt_an_words, Wt_an_scales)),
+    ]
+
+    with ExitStack() as ctx:
+        consts = ctx.enter_context(tc.tile_pool(name="consts", bufs=1))
+        x_pool = ctx.enter_context(tc.tile_pool(name="x_pool", bufs=AHEAD + 2))
+        mx_pool = ctx.enter_context(tc.tile_pool(name="mx_pool", bufs=3))
+        out_pool = ctx.enter_context(tc.tile_pool(name="out_pool", bufs=2))
+        t_psum = ctx.enter_context(tc.psum_pool(name="t_psum", bufs=5))
+        acc_psum = ctx.enter_context(tc.psum_pool(name="acc_psum", bufs=3))
+        ctx.enter_context(tc.manual_schedule())
+
+        ident = consts.tile([P, P], F32)
+        make_identity(nc, ident[:])
+        w_words = consts.tile([P, VIEWS, PASSES, 2 * F], U32, align_bytes=64)
+        w_planes = consts.tile([P, VIEWS, PASSES, 2 * F], U8, align_bytes=64)
+        nc.vector.memset(w_planes[:].rearrange("p v g n -> p (v g n)").bitcast(I32), 0)
+
+        def load_weights(v):
+            for s, (words, scales) in enumerate(weights[v]):
+                cols = slice(s * F, (s + 1) * F)
+                nc.sync.dma_start(
+                    out=w_words[:, v, :, cols].bitcast(I32),
+                    in_=words.rearrange("g p n t -> p g (n t)").bitcast(I32),
+                )
+                for quad in range(QUADRANTS):
+                    nc.sync.dma_start(
+                        out=w_planes[32 * quad : 32 * quad + 4, v, :, cols].bitcast(I32),
+                        in_=scales[:, 4 * quad : 4 * quad + 4, :]
+                        .rearrange("g r n -> r g n")
+                        .bitcast(I32),
+                    )
+
+        def load_x(r):
+            chunk, v = divmod(r, VIEWS)
+            x_sb = x_pool.tile([P, TILES, DIN], BF16)
+            nc.sync.dma_start(out=x_sb[:], in_=x_chunks[v][chunk])
+            return x_sb
+
+        def transpose_and_quantise(x_sb):
+            x_words = x_sb[:].bitcast(F32)
+            grouped = mx_pool.tile([P, TILES, PASSES, P, PACK], BF16, align_bytes=64)
+            grouped_words = grouped[:].bitcast(F32)
+            for j in range(TILES):
+                xt = t_psum.tile([P, PASSES, PAIRS, P], F32)
+                for g in range(PASSES):
+                    for u in range(PAIRS):
+                        nc.tensor.transpose(
+                            xt[:, g, u, :],
+                            x_words[:, j, g * PASS_WORDS + u : (g + 1) * PASS_WORDS : PAIRS],
+                            ident[:],
+                        )
+                nc.scalar.copy(
+                    out=grouped_words[:, j], in_=xt[:].rearrange("p g u b -> p g b u")
+                )
+            codes = mx_pool.tile([P, TILES, PASSES, P], U32, align_bytes=64)
+            planes = mx_pool.tile([P, TILES, PASSES, P], U8, align_bytes=64)
+            for first in range(0, TILES, BANK_TILES):
+                js = slice(first, first + BANK_TILES)
+                nc.vector.quantize_mx(
+                    out=codes[:, js].rearrange("p j g b -> p (j g b)").bitcast(FP8X4),
+                    scales=planes[:, js].rearrange("p j g b -> p (j g b)"),
+                    in_=grouped[:, js].rearrange("p j g b t -> p (j g b t)"),
+                )
+            return codes, planes
+
+        def multiply_and_scale(v, codes, planes, branches):
+            banks = []
+            for first in range(0, TILES, BANK_TILES):
+                acc = acc_psum.tile([P, BANK_TILES, 2, F], F32)
+                for i in range(BANK_TILES):
+                    for g in range(PASSES):
+                        nc.tensor.matmul_mx(
+                            out=acc[:, i].rearrange("p s n -> p (s n)"),
+                            lhsT=codes[:, first + i, g, :].bitcast(FP8X4),
+                            lhsT_scale=planes[:, first + i, g, :],
+                            rhs=w_words[:, v, g, :].bitcast(FP8X4),
+                            rhs_scale=w_planes[:, v, g, :],
+                            start=(g == 0),
+                            stop=(g == PASSES - 1),
+                        )
+                banks.append((first, acc))
+            sums = []
+            for first, acc in banks:
+                an_sum = out_pool.tile([P, BANK_TILES], F32, name="an_sum%d" % first)
+                nc.vector.tensor_reduce(out=an_sum[:], in_=acc[:, :, 1, :], axis=X_AXIS, op=ADD)
+                sums.append(an_sum)
+            for (first, acc), an_sum in zip(banks, sums):
+                nc.vector.scalar_tensor_tensor(
+                    out=branches[:, first : first + BANK_TILES, v * F : (v + 1) * F],
+                    in0=acc[:, :, 0, :],
+                    scalar=1.0 / (F * VIEWS),
+                    in1=an_sum[:].unsqueeze(2).to_broadcast([P, BANK_TILES, F]),
+                    op0=MULT,
+                    op1=MULT,
+                )
+
+        def average_and_store(chunk, branches):
+            result = out_pool.tile([P, TILES, F], F32)
+            nc.vector.tensor_reduce(
+                out=result[:],
+                in_=branches[:].rearrange("p j (n t) -> p j n t", t=VIEWS),
+                axis=X_AXIS,
+                op=ADD,
+            )
+            nc.sync.dma_start(out=out_chunks[chunk], in_=result[:])
+
+        x_tiles = {}
+        for r in range(AHEAD):
+            x_tiles[r] = load_x(r)
+            if r < VIEWS:
+                load_weights(r)
+
+        quantised = {}
+        branches = None
+        for s in range(ROUNDS + 1):
+            if s + AHEAD < ROUNDS:
+                x_tiles[s + AHEAD] = load_x(s + AHEAD)
+            if s < ROUNDS:
+                quantised[s] = transpose_and_quantise(x_tiles[s])
+            if s >= 1:
+                chunk, v = divmod(s - 1, VIEWS)
+                if v == 0:
+                    branches = out_pool.tile([P, TILES, VIEWS * F], F32)
+                codes, planes = quantised[s - 1]
+                multiply_and_scale(v, codes, planes, branches)
+                if v == VIEWS - 1:
+                    average_and_store(chunk, branches)

@@ -12,6 +12,7 @@ FP8X4 = mybir.dt.float8_e4m3fn_x4
 ADD = mybir.AluOpType.add
 MULT = mybir.AluOpType.mult
 X_AXIS = mybir.AxisListType.X
+COPY = mybir.ActivationFunctionType.Copy
 
 P = 128
 PACK = 4
@@ -20,11 +21,13 @@ B, DIN, F, VIEWS = 4096, 1024, 128, 3
 PASSES = DIN // K_PASS
 PAIRS = PACK // 2
 PASS_WORDS = K_PASS // 2
-TILES = 4
+HALF = 2
+HALVES = 2
+TILES = HALF * HALVES
 CHUNKS = B // (P * TILES)
 ROUNDS = CHUNKS * VIEWS
-BANK_TILES = 2
-AHEAD = 4
+LAG = 2
+AHEAD = 6
 QUADRANTS = 4
 
 FLOPS = 2 * 2 * VIEWS * B * DIN * F
@@ -40,9 +43,10 @@ def tile_fusion_r3d_pa_t_kernel(
 ):
     nc = tc.nc
     x_chunks = [
-        x.rearrange("(c p j) k -> c p j k", p=P, j=TILES) for x in (x_dash, x_rear, x_right)
+        x.rearrange("(c p h i) k -> c h p i k", p=P, h=HALVES, i=HALF)
+        for x in (x_dash, x_rear, x_right)
     ]
-    out_chunks = out.rearrange("(c p j) n -> c p j n", p=P, j=TILES)
+    out_chunks = out.rearrange("(c p i) n -> c p i n", p=P, i=TILES)
     weights = [
         ((Wd_nm_words, Wd_nm_scales), (Wd_an_words, Wd_an_scales)),
         ((Wr_nm_words, Wr_nm_scales), (Wr_an_words, Wr_an_scales)),
@@ -52,14 +56,16 @@ def tile_fusion_r3d_pa_t_kernel(
     with ExitStack() as ctx:
         consts = ctx.enter_context(tc.tile_pool(name="consts", bufs=1))
         x_pool = ctx.enter_context(tc.tile_pool(name="x_pool", bufs=AHEAD + 2))
-        mx_pool = ctx.enter_context(tc.tile_pool(name="mx_pool", bufs=3))
-        out_pool = ctx.enter_context(tc.tile_pool(name="out_pool", bufs=2))
-        t_psum = ctx.enter_context(tc.psum_pool(name="t_psum", bufs=5))
-        acc_psum = ctx.enter_context(tc.psum_pool(name="acc_psum", bufs=3))
+        mx_pool = ctx.enter_context(tc.tile_pool(name="mx_pool", bufs=LAG + 2))
+        out_pool = ctx.enter_context(tc.tile_pool(name="out_pool", bufs=3))
+        t_psum = ctx.enter_context(tc.psum_pool(name="t_psum", bufs=TILES))
+        acc_psum = ctx.enter_context(tc.psum_pool(name="acc_psum", bufs=2 * HALVES))
         ctx.enter_context(tc.manual_schedule())
 
         ident = consts.tile([P, P], F32)
         make_identity(nc, ident[:])
+        table_warmer = consts.tile([P, 1], F32)
+        nc.scalar.activation(out=table_warmer[:], in_=ident[:, 0:1], func=COPY)
         w_words = consts.tile([P, VIEWS, PASSES, 2 * F], U32, align_bytes=64)
         w_planes = consts.tile([P, VIEWS, PASSES, 2 * F], U8, align_bytes=64)
         nc.vector.memset(w_planes[:].rearrange("p v g n -> p (v g n)").bitcast(I32), 0)
@@ -81,96 +87,112 @@ def tile_fusion_r3d_pa_t_kernel(
 
         def load_x(r):
             chunk, v = divmod(r, VIEWS)
-            x_sb = x_pool.tile([P, TILES, DIN], BF16)
-            nc.sync.dma_start(out=x_sb[:], in_=x_chunks[v][chunk])
-            return x_sb
+            x_direct = x_pool.tile([P, HALF, DIN], BF16)
+            nc.sync.dma_start(out=x_direct[:], in_=x_chunks[v][chunk, 0])
+            x_unsorted = x_pool.tile([P, HALF, DIN], BF16)
+            nc.sync.dma_start(out=x_unsorted[:], in_=x_chunks[v][chunk, 1])
+            return x_direct, x_unsorted
 
-        def transpose_and_quantise(x_sb):
-            x_words = x_sb[:].bitcast(F32)
-            grouped = mx_pool.tile([P, TILES, PASSES, P, PACK], BF16, align_bytes=64)
+        def sort_words(x_unsorted):
+            x_sorted = mx_pool.tile([P, HALF, PASSES, PAIRS, P], F32)
+            nc.vector.tensor_copy(
+                out=x_sorted[:],
+                in_=x_unsorted[:]
+                .bitcast(F32)
+                .rearrange("p i (g c u) -> p i g u c", g=PASSES, u=PAIRS),
+            )
+            return x_sorted
+
+        def transpose_and_quantise(x_direct, x_sorted):
+            direct_words = x_direct[:].bitcast(F32)
+            grouped = mx_pool.tile([P, HALVES, HALF, PASSES, P, PACK], BF16, align_bytes=64)
             grouped_words = grouped[:].bitcast(F32)
-            for j in range(TILES):
-                xt = t_psum.tile([P, PASSES, PAIRS, P], F32)
-                for g in range(PASSES):
-                    for u in range(PAIRS):
-                        nc.tensor.transpose(
-                            xt[:, g, u, :],
-                            x_words[:, j, g * PASS_WORDS + u : (g + 1) * PASS_WORDS : PAIRS],
-                            ident[:],
-                        )
-                nc.scalar.copy(
-                    out=grouped_words[:, j], in_=xt[:].rearrange("p g u b -> p g b u")
-                )
-            codes = mx_pool.tile([P, TILES, PASSES, P], U32, align_bytes=64)
-            planes = mx_pool.tile([P, TILES, PASSES, P], U8, align_bytes=64)
-            for first in range(0, TILES, BANK_TILES):
-                js = slice(first, first + BANK_TILES)
+            codes = mx_pool.tile([P, HALVES, HALF, PASSES, P], U32, align_bytes=64)
+            planes = mx_pool.tile([P, HALVES, HALF, PASSES, P], U8, align_bytes=64)
+            for h in range(HALVES):
+                for i in range(HALF):
+                    xt = t_psum.tile([P, PASSES, PAIRS, P], F32)
+                    for g in range(PASSES):
+                        for u in range(PAIRS):
+                            if h == 0:
+                                words = direct_words[
+                                    :, i, g * PASS_WORDS + u : (g + 1) * PASS_WORDS : PAIRS
+                                ]
+                            else:
+                                words = x_sorted[:, i, g, u, :]
+                            nc.tensor.transpose(xt[:, g, u, :], words, ident[:])
+                    nc.scalar.copy(
+                        out=grouped_words[:, h, i], in_=xt[:].rearrange("p g u b -> p g b u")
+                    )
                 nc.vector.quantize_mx(
-                    out=codes[:, js].rearrange("p j g b -> p (j g b)").bitcast(FP8X4),
-                    scales=planes[:, js].rearrange("p j g b -> p (j g b)"),
-                    in_=grouped[:, js].rearrange("p j g b t -> p (j g b t)"),
+                    out=codes[:, h].rearrange("p i g b -> p (i g b)").bitcast(FP8X4),
+                    scales=planes[:, h].rearrange("p i g b -> p (i g b)"),
+                    in_=grouped[:, h].rearrange("p i g b t -> p (i g b t)"),
                 )
             return codes, planes
 
         def multiply_and_scale(v, codes, planes, branches):
-            banks = []
-            for first in range(0, TILES, BANK_TILES):
-                acc = acc_psum.tile([P, BANK_TILES, 2, F], F32)
-                for i in range(BANK_TILES):
+            unread = out_pool.tile([P, HALVES, HALF, F], F32)
+            for h in range(HALVES):
+                acc = acc_psum.tile([P, HALF, 2, F], F32)
+                for i in range(HALF):
                     for g in range(PASSES):
                         nc.tensor.matmul_mx(
                             out=acc[:, i].rearrange("p s n -> p (s n)"),
-                            lhsT=codes[:, first + i, g, :].bitcast(FP8X4),
-                            lhsT_scale=planes[:, first + i, g, :],
+                            lhsT=codes[:, h, i, g, :].bitcast(FP8X4),
+                            lhsT_scale=planes[:, h, i, g, :],
                             rhs=w_words[:, v, g, :].bitcast(FP8X4),
                             rhs_scale=w_planes[:, v, g, :],
                             start=(g == 0),
                             stop=(g == PASSES - 1),
                         )
-                banks.append((first, acc))
-            sums = []
-            for first, acc in banks:
-                an_sum = out_pool.tile([P, BANK_TILES], F32, name="an_sum%d" % first)
-                nc.vector.tensor_reduce(out=an_sum[:], in_=acc[:, :, 1, :], axis=X_AXIS, op=ADD)
-                sums.append(an_sum)
-            for (first, acc), an_sum in zip(banks, sums):
-                nc.vector.scalar_tensor_tensor(
-                    out=branches[:, first : first + BANK_TILES, v * F : (v + 1) * F],
+                gate = out_pool.tile([P, HALF], F32, name="gate%d" % h)
+                for i in range(HALF):
+                    nc.scalar.activation(
+                        out=unread[:, h, i, :],
+                        in_=acc[:, i, 1, :],
+                        func=COPY,
+                        scale=1.0 / (F * VIEWS),
+                        accum_out=gate[:, i : i + 1],
+                    )
+                nc.vector.tensor_tensor(
+                    out=branches[:, h * HALF : (h + 1) * HALF, v * F : (v + 1) * F],
                     in0=acc[:, :, 0, :],
-                    scalar=1.0 / (F * VIEWS),
-                    in1=an_sum[:].unsqueeze(2).to_broadcast([P, BANK_TILES, F]),
-                    op0=MULT,
-                    op1=MULT,
+                    in1=gate[:].unsqueeze(2).to_broadcast([P, HALF, F]),
+                    op=MULT,
                 )
 
         def average_and_store(chunk, branches):
             result = out_pool.tile([P, TILES, F], F32)
             nc.vector.tensor_reduce(
                 out=result[:],
-                in_=branches[:].rearrange("p j (n t) -> p j n t", t=VIEWS),
+                in_=branches[:].rearrange("p i (n t) -> p i n t", t=VIEWS),
                 axis=X_AXIS,
                 op=ADD,
             )
             nc.sync.dma_start(out=out_chunks[chunk], in_=result[:])
 
-        x_tiles = {}
+        loaded = {}
         for r in range(AHEAD):
-            x_tiles[r] = load_x(r)
-            if r < VIEWS:
-                load_weights(r)
+            loaded[r] = load_x(r)
+            if r % 2 == 1:
+                load_weights(r // 2)
 
+        sorted_halves = {0: sort_words(loaded[0][1])}
         quantised = {}
         branches = None
-        for s in range(ROUNDS + 1):
+        for s in range(ROUNDS + LAG):
             if s + AHEAD < ROUNDS:
-                x_tiles[s + AHEAD] = load_x(s + AHEAD)
+                loaded[s + AHEAD] = load_x(s + AHEAD)
+            if s + 1 < ROUNDS:
+                sorted_halves[s + 1] = sort_words(loaded[s + 1][1])
             if s < ROUNDS:
-                quantised[s] = transpose_and_quantise(x_tiles[s])
-            if s >= 1:
-                chunk, v = divmod(s - 1, VIEWS)
+                quantised[s] = transpose_and_quantise(loaded[s][0], sorted_halves[s])
+            if s >= LAG:
+                chunk, v = divmod(s - LAG, VIEWS)
                 if v == 0:
                     branches = out_pool.tile([P, TILES, VIEWS * F], F32)
-                codes, planes = quantised[s - 1]
+                codes, planes = quantised[s - LAG]
                 multiply_and_scale(v, codes, planes, branches)
                 if v == VIEWS - 1:
                     average_and_store(chunk, branches)

@@ -103,13 +103,16 @@ def tile_fusion_r3d_pa_t_kernel(
             )
             return x_sorted
 
-        def transpose_and_quantise(x_direct, x_sorted):
-            direct_words = x_direct[:].bitcast(F32)
+        def new_round_tiles():
             grouped = mx_pool.tile([P, HALVES, HALF, PASSES, P, PACK], BF16, align_bytes=64)
-            grouped_words = grouped[:].bitcast(F32)
             codes = mx_pool.tile([P, HALVES, HALF, PASSES, P], U32, align_bytes=64)
             planes = mx_pool.tile([P, HALVES, HALF, PASSES, P], U8, align_bytes=64)
-            for h in range(HALVES):
+            return grouped, codes, planes
+
+        def transpose_and_quantise(h, x_direct, x_sorted, grouped, codes, planes):
+            direct_words = x_direct[:].bitcast(F32)
+            grouped_words = grouped[:].bitcast(F32)
+            if True:
                 for i in range(HALF):
                     xt = t_psum.tile([P, PASSES, PAIRS, P], F32)
                     for g in range(PASSES):
@@ -129,11 +132,10 @@ def tile_fusion_r3d_pa_t_kernel(
                     scales=planes[:, h].rearrange("p i g b -> p (i g b)"),
                     in_=grouped[:, h].rearrange("p i g b t -> p (i g b t)"),
                 )
-            return codes, planes
 
-        def multiply_and_scale(v, codes, planes, branches):
-            unread = out_pool.tile([P, HALVES, HALF, F], F32)
-            for h in range(HALVES):
+        def multiply_and_scale(h, v, codes, planes, branches):
+            unread = out_pool.tile([P, HALVES, HALF, F], F32, name="unread%d" % h)
+            if True:
                 acc = acc_psum.tile([P, HALF, 2, F], F32)
                 for i in range(HALF):
                     for g in range(PASSES):
@@ -187,12 +189,17 @@ def tile_fusion_r3d_pa_t_kernel(
             if s + 1 < ROUNDS:
                 sorted_halves[s + 1] = sort_words(loaded[s + 1][1])
             if s < ROUNDS:
-                quantised[s] = transpose_and_quantise(loaded[s][0], sorted_halves[s])
+                quantised[s] = new_round_tiles()
             if s >= LAG:
                 chunk, v = divmod(s - LAG, VIEWS)
                 if v == 0:
                     branches = out_pool.tile([P, TILES, VIEWS * F], F32)
-                codes, planes = quantised[s - LAG]
-                multiply_and_scale(v, codes, planes, branches)
-                if v == VIEWS - 1:
-                    average_and_store(chunk, branches)
+            for h in range(HALVES):
+                if s < ROUNDS:
+                    grouped, codes, planes = quantised[s]
+                    transpose_and_quantise(h, loaded[s][0], sorted_halves[s], grouped, codes, planes)
+                if s >= LAG:
+                    grouped, codes, planes = quantised[s - LAG]
+                    multiply_and_scale(h, v, codes, planes, branches)
+            if s >= LAG and v == VIEWS - 1:
+                average_and_store(chunk, branches)

@@ -28,6 +28,8 @@ CHUNKS = B // (P * TILES)
 ROUNDS = CHUNKS * VIEWS
 LAG = 2
 AHEAD = 6
+WHOLE = (F - 2) // VIEWS
+BEATS_TO_PASSES = HALVES * LAG
 QUADRANTS = 4
 
 FLOPS = 2 * 2 * VIEWS * B * DIN * F
@@ -133,8 +135,8 @@ def tile_fusion_r3d_pa_t_kernel(
                     in_=grouped[:, h].rearrange("p i g b t -> p (i g b t)"),
                 )
 
-        def multiply_and_scale(h, v, codes, planes, branches):
-            unread = out_pool.tile([P, HALVES, HALF, F], F32, name="unread%d" % h)
+        def multiply(h, v, codes, planes, gate):
+            unread = out_pool.tile([P, HALF, F], F32, name="unread%d" % h)
             if True:
                 acc = acc_psum.tile([P, HALF, 2, F], F32)
                 for i in range(HALF):
@@ -148,27 +150,47 @@ def tile_fusion_r3d_pa_t_kernel(
                             start=(g == 0),
                             stop=(g == PASSES - 1),
                         )
-                gate = out_pool.tile([P, HALF], F32, name="gate%d" % h)
                 for i in range(HALF):
                     nc.scalar.activation(
-                        out=unread[:, h, i, :],
+                        out=unread[:, i, :],
                         in_=acc[:, i, 1, :],
                         func=COPY,
                         scale=1.0 / (F * VIEWS),
-                        accum_out=gate[:, i : i + 1],
+                        accum_out=gate[:, h * HALF + i : h * HALF + i + 1],
                     )
+            return acc
+
+        def sum_up(h, v, acc, gate, sums, edges):
+            rows = slice(h * HALF, (h + 1) * HALF)
+            if True:
+                nc.vector.tensor_reduce(
+                    out=sums[:, rows, :],
+                    in_=acc[:, :, 0, v : v + VIEWS * WHOLE].rearrange(
+                        "p i (m t) -> p i m t", t=VIEWS
+                    ),
+                    axis=X_AXIS,
+                    op=ADD,
+                )
+                first, last = [n for n in range(F) if not v <= n < v + VIEWS * WHOLE]
                 nc.vector.tensor_tensor(
-                    out=branches[:, h * HALF : (h + 1) * HALF, v * F : (v + 1) * F],
-                    in0=acc[:, :, 0, :],
-                    in1=gate[:].unsqueeze(2).to_broadcast([P, HALF, F]),
+                    out=edges[:, rows, 2 * v : 2 * v + 2],
+                    in0=acc[:, :, 0, first : last + 1 : last - first],
+                    in1=gate[:, rows].unsqueeze(2).to_broadcast([P, HALF, 2]),
                     op=MULT,
                 )
 
-        def average_and_store(chunk, branches):
-            result = out_pool.tile([P, TILES, F], F32)
+        def scale_sums(v, gate, sums, result):
+            nc.vector.tensor_tensor(
+                out=result[:, :, (WHOLE + 1) * v : (WHOLE + 1) * v + WHOLE],
+                in0=sums[:],
+                in1=gate[:].unsqueeze(2).to_broadcast([P, TILES, WHOLE]),
+                op=MULT,
+            )
+
+        def finish_and_store(chunk, edges, result):
             nc.vector.tensor_reduce(
-                out=result[:],
-                in_=branches[:].rearrange("p i (n t) -> p i n t", t=VIEWS),
+                out=result[:, :, WHOLE : F : WHOLE + 1],
+                in_=edges[:].rearrange("p i (e t) -> p i e t", t=VIEWS),
                 axis=X_AXIS,
                 op=ADD,
             )
@@ -182,24 +204,42 @@ def tile_fusion_r3d_pa_t_kernel(
 
         sorted_halves = {0: sort_words(loaded[0][1])}
         quantised = {}
-        branches = None
-        for s in range(ROUNDS + LAG):
-            if s + AHEAD < ROUNDS:
-                loaded[s + AHEAD] = load_x(s + AHEAD)
-            if s + 1 < ROUNDS:
-                sorted_halves[s + 1] = sort_words(loaded[s + 1][1])
-            if s < ROUNDS:
-                quantised[s] = new_round_tiles()
-            if s >= LAG:
-                chunk, v = divmod(s - LAG, VIEWS)
-                if v == 0:
-                    branches = out_pool.tile([P, TILES, VIEWS * F], F32)
-            for h in range(HALVES):
-                if s < ROUNDS:
-                    grouped, codes, planes = quantised[s]
-                    transpose_and_quantise(h, loaded[s][0], sorted_halves[s], grouped, codes, planes)
-                if s >= LAG:
-                    grouped, codes, planes = quantised[s - LAG]
-                    multiply_and_scale(h, v, codes, planes, branches)
-            if s >= LAG and v == VIEWS - 1:
-                average_and_store(chunk, branches)
+        epilogue = {}
+        outputs = {}
+        products = {}
+        for k in range(HALVES * ROUNDS + BEATS_TO_PASSES + 1):
+            r, h = divmod(k, HALVES)
+            if h == 0:
+                if r + AHEAD < ROUNDS:
+                    loaded[r + AHEAD] = load_x(r + AHEAD)
+                if r + 1 < ROUNDS:
+                    sorted_halves[r + 1] = sort_words(loaded[r + 1][1])
+                if r < ROUNDS:
+                    quantised[r] = new_round_tiles()
+            if 0 <= k - BEATS_TO_PASSES - 1:
+                r_out, h_out = divmod(k - BEATS_TO_PASSES - 1, HALVES)
+                chunk, v = divmod(r_out, VIEWS)
+                gate, sums = epilogue[r_out]
+                edges, result = outputs[chunk]
+                sum_up(h_out, v, products[k - BEATS_TO_PASSES - 1], gate, sums, edges)
+                if h_out == HALVES - 1:
+                    scale_sums(v, gate, sums, result)
+                    if v == VIEWS - 1:
+                        finish_and_store(chunk, edges, result)
+            if r < ROUNDS:
+                grouped, codes, planes = quantised[r]
+                transpose_and_quantise(h, loaded[r][0], sorted_halves[r], grouped, codes, planes)
+            if 0 <= k - BEATS_TO_PASSES < HALVES * ROUNDS:
+                r_mul, h_mul = divmod(k - BEATS_TO_PASSES, HALVES)
+                if h_mul == 0:
+                    if r_mul % VIEWS == 0:
+                        edges = out_pool.tile([P, TILES, 2 * VIEWS], F32)
+                        result = out_pool.tile([P, TILES, F], F32)
+                        outputs[r_mul // VIEWS] = (edges, result)
+                    gate = out_pool.tile([P, TILES], F32)
+                    sums = out_pool.tile([P, TILES, WHOLE], F32)
+                    epilogue[r_mul] = (gate, sums)
+                grouped, codes, planes = quantised[r_mul]
+                products[k - BEATS_TO_PASSES] = multiply(
+                    h_mul, r_mul % VIEWS, codes, planes, epilogue[r_mul][0]
+                )

@@ -29,7 +29,9 @@ ROUNDS = CHUNKS * VIEWS
 LAG = 2
 AHEAD = 6
 WHOLE = (F - 2) // VIEWS
-BEATS_TO_PASSES = HALVES * LAG
+GROUP = 2
+BEATS = HALVES * ROUNDS // GROUP
+BEATS_TO_PASSES = HALVES * LAG // GROUP
 QUADRANTS = 4
 
 FLOPS = 2 * 2 * VIEWS * B * DIN * F
@@ -207,39 +209,46 @@ def tile_fusion_r3d_pa_t_kernel(
         epilogue = {}
         outputs = {}
         products = {}
-        for k in range(HALVES * ROUNDS + BEATS_TO_PASSES + 1):
-            r, h = divmod(k, HALVES)
-            if h == 0:
-                if r + AHEAD < ROUNDS:
-                    loaded[r + AHEAD] = load_x(r + AHEAD)
-                if r + 1 < ROUNDS:
-                    sorted_halves[r + 1] = sort_words(loaded[r + 1][1])
-                if r < ROUNDS:
-                    quantised[r] = new_round_tiles()
+        for k in range(BEATS + BEATS_TO_PASSES + 1):
+            for half in range(GROUP * k, GROUP * (k + 1)):
+                r, h = divmod(half, HALVES)
+                if h == 0:
+                    if r + AHEAD < ROUNDS:
+                        loaded[r + AHEAD] = load_x(r + AHEAD)
+                    if r + 1 < ROUNDS:
+                        sorted_halves[r + 1] = sort_words(loaded[r + 1][1])
+                    if r < ROUNDS:
+                        quantised[r] = new_round_tiles()
             if 0 <= k - BEATS_TO_PASSES - 1:
-                r_out, h_out = divmod(k - BEATS_TO_PASSES - 1, HALVES)
-                chunk, v = divmod(r_out, VIEWS)
-                gate, sums = epilogue[r_out]
-                edges, result = outputs[chunk]
-                sum_up(h_out, v, products[k - BEATS_TO_PASSES - 1], gate, sums, edges)
-                if h_out == HALVES - 1:
-                    scale_sums(v, gate, sums, result)
-                    if v == VIEWS - 1:
-                        finish_and_store(chunk, edges, result)
-            if r < ROUNDS:
-                grouped, codes, planes = quantised[r]
-                transpose_and_quantise(h, loaded[r][0], sorted_halves[r], grouped, codes, planes)
-            if 0 <= k - BEATS_TO_PASSES < HALVES * ROUNDS:
-                r_mul, h_mul = divmod(k - BEATS_TO_PASSES, HALVES)
-                if h_mul == 0:
-                    if r_mul % VIEWS == 0:
-                        edges = out_pool.tile([P, TILES, 2 * VIEWS], F32)
-                        result = out_pool.tile([P, TILES, F], F32)
-                        outputs[r_mul // VIEWS] = (edges, result)
-                    gate = out_pool.tile([P, TILES], F32)
-                    sums = out_pool.tile([P, TILES, WHOLE], F32)
-                    epilogue[r_mul] = (gate, sums)
-                grouped, codes, planes = quantised[r_mul]
-                products[k - BEATS_TO_PASSES] = multiply(
-                    h_mul, r_mul % VIEWS, codes, planes, epilogue[r_mul][0]
-                )
+                for half in range(GROUP * (k - BEATS_TO_PASSES - 1), GROUP * (k - BEATS_TO_PASSES)):
+                    r_out, h_out = divmod(half, HALVES)
+                    chunk, v = divmod(r_out, VIEWS)
+                    gate, sums = epilogue[r_out]
+                    edges, result = outputs[chunk]
+                    sum_up(h_out, v, products[half], gate, sums, edges)
+                    if h_out == HALVES - 1:
+                        scale_sums(v, gate, sums, result)
+                        if v == VIEWS - 1:
+                            finish_and_store(chunk, edges, result)
+            if k < BEATS:
+                for half in range(GROUP * k, GROUP * (k + 1)):
+                    r, h = divmod(half, HALVES)
+                    grouped, codes, planes = quantised[r]
+                    transpose_and_quantise(
+                        h, loaded[r][0], sorted_halves[r], grouped, codes, planes
+                    )
+            if 0 <= k - BEATS_TO_PASSES < BEATS:
+                for half in range(GROUP * (k - BEATS_TO_PASSES), GROUP * (k - BEATS_TO_PASSES + 1)):
+                    r_mul, h_mul = divmod(half, HALVES)
+                    if h_mul == 0:
+                        if r_mul % VIEWS == 0:
+                            edges = out_pool.tile([P, TILES, 2 * VIEWS], F32)
+                            result = out_pool.tile([P, TILES, F], F32)
+                            outputs[r_mul // VIEWS] = (edges, result)
+                        gate = out_pool.tile([P, TILES], F32)
+                        sums = out_pool.tile([P, TILES, WHOLE], F32)
+                        epilogue[r_mul] = (gate, sums)
+                    grouped, codes, planes = quantised[r_mul]
+                    products[half] = multiply(
+                        h_mul, r_mul % VIEWS, codes, planes, epilogue[r_mul][0]
+                    )

@@ -29,6 +29,7 @@ ROUNDS = CHUNKS * VIEWS
 LAG = 2
 AHEAD = 6
 WHOLE = (F - 2) // VIEWS
+WEAVE = 3
 GROUP = 2
 BEATS = HALVES * ROUNDS // GROUP
 BEATS_TO_PASSES = HALVES * LAG // GROUP
@@ -74,27 +75,40 @@ def tile_fusion_r3d_pa_t_kernel(
         w_planes = consts.tile([P, VIEWS, PASSES, 2 * F], U8, align_bytes=64)
         nc.vector.memset(w_planes[:].rearrange("p v g n -> p (v g n)").bitcast(I32), 0)
 
-        def load_weights(v):
-            for s, (words, scales) in enumerate(weights[v]):
-                cols = slice(s * F, (s + 1) * F)
+        def load_weight_piece(v, s, quad):
+            words, scales = weights[v][s]
+            cols = slice(s * F, (s + 1) * F)
+            if quad < 0:
                 nc.sync.dma_start(
                     out=w_words[:, v, :, cols].bitcast(I32),
                     in_=words.rearrange("g p n t -> p g (n t)").bitcast(I32),
                 )
-                for quad in range(QUADRANTS):
-                    nc.sync.dma_start(
-                        out=w_planes[32 * quad : 32 * quad + 4, v, :, cols].bitcast(I32),
-                        in_=scales[:, 4 * quad : 4 * quad + 4, :]
-                        .rearrange("g r n -> r g n")
-                        .bitcast(I32),
-                    )
+            else:
+                nc.sync.dma_start(
+                    out=w_planes[32 * quad : 32 * quad + 4, v, :, cols].bitcast(I32),
+                    in_=scales[:, 4 * quad : 4 * quad + 4, :]
+                    .rearrange("g r n -> r g n")
+                    .bitcast(I32),
+                )
+
+        pieces = [
+            (v, s, quad) for v in range(VIEWS) for s in range(2) for quad in range(-1, QUADRANTS)
+        ]
+        queued = {"pieces": 0}
+
+        def weave_weights():
+            for piece in pieces[queued["pieces"] : queued["pieces"] + WEAVE]:
+                load_weight_piece(*piece)
+            queued["pieces"] = queued["pieces"] + WEAVE
 
         def load_x(r):
             chunk, v = divmod(r, VIEWS)
             x_direct = x_pool.tile([P, HALF, DIN], BF16)
             nc.sync.dma_start(out=x_direct[:], in_=x_chunks[v][chunk, 0])
+            weave_weights()
             x_unsorted = x_pool.tile([P, HALF, DIN], BF16)
             nc.sync.dma_start(out=x_unsorted[:], in_=x_chunks[v][chunk, 1])
+            weave_weights()
             return x_direct, x_unsorted
 
         def sort_words(x_unsorted):
@@ -201,8 +215,6 @@ def tile_fusion_r3d_pa_t_kernel(
         loaded = {}
         for r in range(AHEAD):
             loaded[r] = load_x(r)
-            if r % 2 == 1:
-                load_weights(r // 2)
 
         sorted_halves = {0: sort_words(loaded[0][1])}
         quantised = {}

@@ -29,7 +29,7 @@ ROUNDS = CHUNKS * VIEWS
 LAG = 2
 AHEAD = 6
 WHOLE = (F - 2) // VIEWS
-WEAVE = 3
+WEAVE = 2
 GROUP = 2
 BEATS = HALVES * ROUNDS // GROUP
 BEATS_TO_PASSES = HALVES * LAG // GROUP
@@ -102,23 +102,27 @@ def tile_fusion_r3d_pa_t_kernel(
             queued["pieces"] = queued["pieces"] + WEAVE
 
         def load_x(r):
-            chunk, v = divmod(r, VIEWS)
+            v, chunk = divmod(r, CHUNKS)
             x_direct = x_pool.tile([P, HALF, DIN], BF16)
-            nc.sync.dma_start(out=x_direct[:], in_=x_chunks[v][chunk, 0])
-            weave_weights()
             x_unsorted = x_pool.tile([P, HALF, DIN], BF16)
-            nc.sync.dma_start(out=x_unsorted[:], in_=x_chunks[v][chunk, 1])
-            weave_weights()
+            for h, x_half in enumerate((x_direct, x_unsorted)):
+                step = 1 if r == 0 else HALF
+                for i in range(0, HALF, step):
+                    nc.sync.dma_start(
+                        out=x_half[:, i : i + step], in_=x_chunks[v][chunk, h, :, i : i + step]
+                    )
+                weave_weights()
             return x_direct, x_unsorted
 
-        def sort_words(x_unsorted):
+        def sort_words(x_unsorted, step):
             x_sorted = mx_pool.tile([P, HALF, PASSES, PAIRS, P], F32)
-            nc.vector.tensor_copy(
-                out=x_sorted[:],
-                in_=x_unsorted[:]
-                .bitcast(F32)
-                .rearrange("p i (g c u) -> p i g u c", g=PASSES, u=PAIRS),
-            )
+            for i in range(0, HALF, step):
+                nc.vector.tensor_copy(
+                    out=x_sorted[:, i : i + step],
+                    in_=x_unsorted[:, i : i + step]
+                    .bitcast(F32)
+                    .rearrange("p i (g c u) -> p i g u c", g=PASSES, u=PAIRS),
+                )
             return x_sorted
 
         def new_round_tiles():
@@ -206,20 +210,21 @@ def tile_fusion_r3d_pa_t_kernel(
         def finish_and_store(chunk, edges, result):
             nc.vector.tensor_reduce(
                 out=result[:, :, WHOLE : F : WHOLE + 1],
-                in_=edges[:].rearrange("p i (e t) -> p i e t", t=VIEWS),
+                in_=edges.rearrange("p i (e t) -> p i e t", t=VIEWS),
                 axis=X_AXIS,
                 op=ADD,
             )
-            nc.sync.dma_start(out=out_chunks[chunk], in_=result[:])
+            nc.sync.dma_start(out=out_chunks[chunk], in_=result)
 
         loaded = {}
         for r in range(AHEAD):
             loaded[r] = load_x(r)
 
-        sorted_halves = {0: sort_words(loaded[0][1])}
+        sorted_halves = {0: sort_words(loaded[0][1], 1)}
         quantised = {}
         epilogue = {}
-        outputs = {}
+        all_edges = consts.tile([P, CHUNKS, TILES, 2 * VIEWS], F32)
+        all_results = consts.tile([P, CHUNKS, TILES, F], F32)
         products = {}
         for k in range(BEATS + BEATS_TO_PASSES + 1):
             for half in range(GROUP * k, GROUP * (k + 1)):
@@ -228,15 +233,16 @@ def tile_fusion_r3d_pa_t_kernel(
                     if r + AHEAD < ROUNDS:
                         loaded[r + AHEAD] = load_x(r + AHEAD)
                     if r + 1 < ROUNDS:
-                        sorted_halves[r + 1] = sort_words(loaded[r + 1][1])
+                        sorted_halves[r + 1] = sort_words(loaded[r + 1][1], HALF)
                     if r < ROUNDS:
                         quantised[r] = new_round_tiles()
             if 0 <= k - BEATS_TO_PASSES - 1:
                 for half in range(GROUP * (k - BEATS_TO_PASSES - 1), GROUP * (k - BEATS_TO_PASSES)):
                     r_out, h_out = divmod(half, HALVES)
-                    chunk, v = divmod(r_out, VIEWS)
+                    v, chunk = divmod(r_out, CHUNKS)
                     gate, sums = epilogue[r_out]
-                    edges, result = outputs[chunk]
+                    edges = all_edges[:, chunk]
+                    result = all_results[:, chunk]
                     sum_up(h_out, v, products[half], gate, sums, edges)
                     if h_out == HALVES - 1:
                         scale_sums(v, gate, sums, result)
@@ -253,14 +259,10 @@ def tile_fusion_r3d_pa_t_kernel(
                 for half in range(GROUP * (k - BEATS_TO_PASSES), GROUP * (k - BEATS_TO_PASSES + 1)):
                     r_mul, h_mul = divmod(half, HALVES)
                     if h_mul == 0:
-                        if r_mul % VIEWS == 0:
-                            edges = out_pool.tile([P, TILES, 2 * VIEWS], F32)
-                            result = out_pool.tile([P, TILES, F], F32)
-                            outputs[r_mul // VIEWS] = (edges, result)
                         gate = out_pool.tile([P, TILES], F32)
                         sums = out_pool.tile([P, TILES, WHOLE], F32)
                         epilogue[r_mul] = (gate, sums)
                     grouped, codes, planes = quantised[r_mul]
                     products[half] = multiply(
-                        h_mul, r_mul % VIEWS, codes, planes, epilogue[r_mul][0]
+                        h_mul, r_mul // CHUNKS, codes, planes, epilogue[r_mul][0]
                     )

@@ -96,10 +96,11 @@ def tile_fusion_r3d_pa_t_kernel(
         ]
         queued = {"pieces": 0}
 
-        def weave_weights():
-            for piece in pieces[queued["pieces"] : queued["pieces"] + WEAVE]:
+        def weave_weights(views_wanted):
+            upto = min(queued["pieces"] + WEAVE, views_wanted * len(pieces) // VIEWS)
+            for piece in pieces[queued["pieces"] : upto]:
                 load_weight_piece(*piece)
-            queued["pieces"] = queued["pieces"] + WEAVE
+            queued["pieces"] = max(queued["pieces"], upto)
 
         def load_x(r):
             v, chunk = divmod(r, CHUNKS)
@@ -111,7 +112,7 @@ def tile_fusion_r3d_pa_t_kernel(
                     nc.sync.dma_start(
                         out=x_half[:, i : i + step], in_=x_chunks[v][chunk, h, :, i : i + step]
                     )
-                weave_weights()
+                weave_weights(1 if r < AHEAD else VIEWS)
             return x_direct, x_unsorted
 
         def sort_words(x_unsorted, step):

@@ -29,13 +29,16 @@ ROUNDS = CHUNKS * VIEWS
 LAG = 2
 AHEAD = 6
 WHOLE = (F - 2) // VIEWS
+LAST_BEFORE_END = ROUNDS - LAG - 2
+LIGHT_FROM = ROUNDS - 4
 WEAVE = 2
-GROUP = 2
-BEATS = HALVES * ROUNDS // GROUP
-BEATS_TO_PASSES = HALVES * LAG // GROUP
 QUADRANTS = 4
 
 FLOPS = 2 * 2 * VIEWS * B * DIN * F
+
+
+def sorted_tiles(r):
+    return 3 if r % 2 == 1 and LAG < r < LIGHT_FROM else 2
 
 
 def tile_fusion_r3d_pa_t_kernel(
@@ -48,7 +51,7 @@ def tile_fusion_r3d_pa_t_kernel(
 ):
     nc = tc.nc
     x_chunks = [
-        x.rearrange("(c p h i) k -> c h p i k", p=P, h=HALVES, i=HALF)
+        x.rearrange("(c p i) k -> c p i k", p=P, i=TILES)
         for x in (x_dash, x_rear, x_right)
     ]
     out_chunks = out.rearrange("(c p i) n -> c p i n", p=P, i=TILES)
@@ -104,166 +107,188 @@ def tile_fusion_r3d_pa_t_kernel(
 
         def load_x(r):
             v, chunk = divmod(r, CHUNKS)
-            x_direct = x_pool.tile([P, HALF, DIN], BF16)
-            x_unsorted = x_pool.tile([P, HALF, DIN], BF16)
-            for h, x_half in enumerate((x_direct, x_unsorted)):
+            x_round = x_pool.tile([P, TILES, DIN], BF16)
+            for h in range(HALVES):
                 step = 1 if r == 0 else HALF
-                for i in range(0, HALF, step):
+                for i in range(h * HALF, (h + 1) * HALF, step):
                     nc.sync.dma_start(
-                        out=x_half[:, i : i + step], in_=x_chunks[v][chunk, h, :, i : i + step]
+                        out=x_round[:, i : i + step], in_=x_chunks[v][chunk, :, i : i + step]
                     )
                 weave_weights(1 if r < AHEAD else VIEWS)
-            return x_direct, x_unsorted
+            loaded[r] = x_round
 
-        def sort_words(x_unsorted, step):
-            x_sorted = mx_pool.tile([P, HALF, PASSES, PAIRS, P], F32)
-            for i in range(0, HALF, step):
+        def sort_words(r):
+            count = sorted_tiles(r)
+            x_sorted = mx_pool.tile([P, PASSES, count, PAIRS, P], F32, name="x_sorted")
+            step = 1 if r == 0 else count
+            for i in range(0, count, step):
+                first = TILES - count + i
                 nc.vector.tensor_copy(
-                    out=x_sorted[:, i : i + step],
-                    in_=x_unsorted[:, i : i + step]
+                    out=x_sorted[:, :, i : i + step],
+                    in_=loaded[r][:, first : first + step]
                     .bitcast(F32)
-                    .rearrange("p i (g c u) -> p i g u c", g=PASSES, u=PAIRS),
+                    .rearrange("p i (g c u) -> p g i u c", g=PASSES, u=PAIRS),
                 )
-            return x_sorted
+            sorted_words[r] = x_sorted
 
-        def new_round_tiles():
+        def new_round_tiles(r):
             grouped = mx_pool.tile([P, HALVES, HALF, PASSES, P, PACK], BF16, align_bytes=64)
             codes = mx_pool.tile([P, HALVES, HALF, PASSES, P], U32, align_bytes=64)
             planes = mx_pool.tile([P, HALVES, HALF, PASSES, P], U8, align_bytes=64)
-            return grouped, codes, planes
+            quantised[r] = (grouped, codes, planes)
 
-        def transpose_and_quantise(h, x_direct, x_sorted, grouped, codes, planes):
-            direct_words = x_direct[:].bitcast(F32)
+        def transpose(r, h):
+            grouped = quantised[r][0]
+            direct_words = loaded[r][:].bitcast(F32)
+            first_sorted = TILES - sorted_tiles(r)
             grouped_words = grouped[:].bitcast(F32)
-            if True:
-                for i in range(HALF):
-                    xt = t_psum.tile([P, PASSES, PAIRS, P], F32)
-                    for g in range(PASSES):
-                        for u in range(PAIRS):
-                            if h == 0:
-                                words = direct_words[
-                                    :, i, g * PASS_WORDS + u : (g + 1) * PASS_WORDS : PAIRS
-                                ]
-                            else:
-                                words = x_sorted[:, i, g, u, :]
-                            nc.tensor.transpose(xt[:, g, u, :], words, ident[:])
-                    nc.scalar.copy(
-                        out=grouped_words[:, h, i], in_=xt[:].rearrange("p g u b -> p g b u")
-                    )
-                nc.vector.quantize_mx(
-                    out=codes[:, h].rearrange("p i g b -> p (i g b)").bitcast(FP8X4),
-                    scales=planes[:, h].rearrange("p i g b -> p (i g b)"),
-                    in_=grouped[:, h].rearrange("p i g b t -> p (i g b t)"),
+            for i in range(HALF):
+                xt = t_psum.tile([P, PASSES, PAIRS, P], F32)
+                for g in range(PASSES):
+                    for u in range(PAIRS):
+                        tile = h * HALF + i
+                        if tile < first_sorted:
+                            words = direct_words[
+                                :, tile, g * PASS_WORDS + u : (g + 1) * PASS_WORDS : PAIRS
+                            ]
+                        else:
+                            words = sorted_words[r][:, g, tile - first_sorted, u, :]
+                        nc.tensor.transpose(xt[:, g, u, :], words, ident[:])
+                nc.scalar.copy(
+                    out=grouped_words[:, h, i], in_=xt[:].rearrange("p g u b -> p g b u")
                 )
 
-        def multiply(h, v, codes, planes, gate):
-            unread = out_pool.tile([P, HALF, F], F32, name="unread%d" % h)
-            if True:
-                acc = acc_psum.tile([P, HALF, 2, F], F32)
-                for i in range(HALF):
-                    for g in range(PASSES):
-                        nc.tensor.matmul_mx(
-                            out=acc[:, i].rearrange("p s n -> p (s n)"),
-                            lhsT=codes[:, h, i, g, :].bitcast(FP8X4),
-                            lhsT_scale=planes[:, h, i, g, :],
-                            rhs=w_words[:, v, g, :].bitcast(FP8X4),
-                            rhs_scale=w_planes[:, v, g, :],
-                            start=(g == 0),
-                            stop=(g == PASSES - 1),
-                        )
-                for i in range(HALF):
-                    nc.scalar.activation(
-                        out=unread[:, i, :],
-                        in_=acc[:, i, 1, :],
-                        func=COPY,
-                        scale=1.0 / (F * VIEWS),
-                        accum_out=gate[:, h * HALF + i : h * HALF + i + 1],
-                    )
-            return acc
-
-        def sum_up(h, v, acc, gate, sums, edges):
-            rows = slice(h * HALF, (h + 1) * HALF)
-            if True:
-                nc.vector.tensor_reduce(
-                    out=sums[:, rows, :],
-                    in_=acc[:, :, 0, v : v + VIEWS * WHOLE].rearrange(
-                        "p i (m t) -> p i m t", t=VIEWS
-                    ),
-                    axis=X_AXIS,
-                    op=ADD,
-                )
-                first, last = [n for n in range(F) if not v <= n < v + VIEWS * WHOLE]
-                nc.vector.tensor_tensor(
-                    out=edges[:, rows, 2 * v : 2 * v + 2],
-                    in0=acc[:, :, 0, first : last + 1 : last - first],
-                    in1=gate[:, rows].unsqueeze(2).to_broadcast([P, HALF, 2]),
-                    op=MULT,
-                )
-
-        def scale_sums(v, gate, sums, result):
-            nc.vector.tensor_tensor(
-                out=result[:, :, (WHOLE + 1) * v : (WHOLE + 1) * v + WHOLE],
-                in0=sums[:],
-                in1=gate[:].unsqueeze(2).to_broadcast([P, TILES, WHOLE]),
-                op=MULT,
+        def quantise(r, halves):
+            grouped, codes, planes = quantised[r]
+            nc.vector.quantize_mx(
+                out=codes[:, halves].rearrange("p h i g b -> p (h i g b)").bitcast(FP8X4),
+                scales=planes[:, halves].rearrange("p h i g b -> p (h i g b)"),
+                in_=grouped[:, halves].rearrange("p h i g b t -> p (h i g b t)"),
             )
 
-        def finish_and_store(chunk, edges, result):
+        def multiply(r, h):
+            codes, planes = quantised[r][1:]
+            v = r // CHUNKS
+            if r == ROUNDS - 1:
+                xt = t_psum.tile([P, PASSES, PAIRS, P], F32)
+                acc = xt
+            else:
+                acc = acc_psum.tile([P, HALF, 2, F], F32)
+            for i in range(HALF):
+                for g in range(PASSES):
+                    nc.tensor.matmul_mx(
+                        out=acc[:, i].rearrange("p s n -> p (s n)"),
+                        lhsT=codes[:, h, i, g, :].bitcast(FP8X4),
+                        lhsT_scale=planes[:, h, i, g, :],
+                        rhs=w_words[:, v, g, :].bitcast(FP8X4),
+                        rhs_scale=w_planes[:, v, g, :],
+                        start=(g == 0),
+                        stop=(g == PASSES - 1),
+                    )
+            products[r, h] = acc
+
+        def new_epilogue_tiles(r):
+            gate = out_pool.tile([P, TILES], F32)
+            sums = out_pool.tile([P, TILES, WHOLE], F32)
+            epilogue[r] = (gate, sums)
+
+        def vector_sums_an(r, h):
+            return h == 1 and r % 2 == 0 and r < LIGHT_FROM - 2
+
+        def sum_an(r, h):
+            acc = products[r, h]
+            gate = epilogue[r][0]
+            if vector_sums_an(r, h):
+                return
+            unread = out_pool.tile([P, HALF, F], F32, name="unread%d" % h)
+            for i in range(HALF):
+                nc.scalar.activation(
+                    out=unread[:, i, :],
+                    in_=acc[:, i, 1, :],
+                    func=COPY,
+                    accum_out=gate[:, h * HALF + i : h * HALF + i + 1],
+                )
+
+        def sum_up(r, h):
+            v, chunk = divmod(r, CHUNKS)
+            acc = products[r, h]
+            gate, sums = epilogue[r]
+            rows = slice(h * HALF, (h + 1) * HALF)
+            if vector_sums_an(r, h):
+                nc.vector.tensor_reduce(out=gate[:, rows], in_=acc[:, :, 1, :], axis=X_AXIS, op=ADD)
             nc.vector.tensor_reduce(
-                out=result[:, :, WHOLE : F : WHOLE + 1],
-                in_=edges.rearrange("p i (e t) -> p i e t", t=VIEWS),
+                out=sums[:, rows, :],
+                in_=acc[:, :, 0, v : v + VIEWS * WHOLE].rearrange("p i (m t) -> p i m t", t=VIEWS),
                 axis=X_AXIS,
                 op=ADD,
             )
-            nc.sync.dma_start(out=out_chunks[chunk], in_=result)
+            first, last = [n for n in range(F) if not v <= n < v + VIEWS * WHOLE]
+            nc.vector.scalar_tensor_tensor(
+                out=all_edges[:, chunk, rows, 2 * v : 2 * v + 2],
+                in0=acc[:, :, 0, first : last + 1 : last - first],
+                scalar=1.0 / (F * VIEWS),
+                in1=gate[:, rows].unsqueeze(2).to_broadcast([P, HALF, 2]),
+                op0=MULT,
+                op1=MULT,
+            )
+
+        def finish(r, rows):
+            v, chunk = divmod(r, CHUNKS)
+            gate, sums = epilogue[r]
+            result = all_results[:, chunk, rows]
+            nc.vector.scalar_tensor_tensor(
+                out=result[:, :, (WHOLE + 1) * v : (WHOLE + 1) * v + WHOLE],
+                in0=sums[:, rows],
+                scalar=1.0 / (F * VIEWS),
+                in1=gate[:, rows].unsqueeze(2).to_broadcast([P, rows.stop - rows.start, WHOLE]),
+                op0=MULT,
+                op1=MULT,
+            )
+            if v == VIEWS - 1:
+                nc.vector.tensor_reduce(
+                    out=result[:, :, WHOLE : F : WHOLE + 1],
+                    in_=all_edges[:, chunk, rows].rearrange("p i (e t) -> p i e t", t=VIEWS),
+                    axis=X_AXIS,
+                    op=ADD,
+                )
+                nc.sync.dma_start(out=out_chunks[chunk][:, rows], in_=result)
 
         loaded = {}
-        for r in range(AHEAD):
-            loaded[r] = load_x(r)
-
-        sorted_halves = {0: sort_words(loaded[0][1], 1)}
+        sorted_words = {}
         quantised = {}
+        products = {}
         epilogue = {}
         all_edges = consts.tile([P, CHUNKS, TILES, 2 * VIEWS], F32)
         all_results = consts.tile([P, CHUNKS, TILES, F], F32)
-        products = {}
-        for k in range(BEATS + BEATS_TO_PASSES + 1):
-            for half in range(GROUP * k, GROUP * (k + 1)):
-                r, h = divmod(half, HALVES)
-                if h == 0:
-                    if r + AHEAD < ROUNDS:
-                        loaded[r + AHEAD] = load_x(r + AHEAD)
-                    if r + 1 < ROUNDS:
-                        sorted_halves[r + 1] = sort_words(loaded[r + 1][1], HALF)
-                    if r < ROUNDS:
-                        quantised[r] = new_round_tiles()
-            if 0 <= k - BEATS_TO_PASSES - 1:
-                for half in range(GROUP * (k - BEATS_TO_PASSES - 1), GROUP * (k - BEATS_TO_PASSES)):
-                    r_out, h_out = divmod(half, HALVES)
-                    v, chunk = divmod(r_out, CHUNKS)
-                    gate, sums = epilogue[r_out]
-                    edges = all_edges[:, chunk]
-                    result = all_results[:, chunk]
-                    sum_up(h_out, v, products[half], gate, sums, edges)
-                    if h_out == HALVES - 1:
-                        scale_sums(v, gate, sums, result)
-                        if v == VIEWS - 1:
-                            finish_and_store(chunk, edges, result)
-            if k < BEATS:
-                for half in range(GROUP * k, GROUP * (k + 1)):
-                    r, h = divmod(half, HALVES)
-                    grouped, codes, planes = quantised[r]
-                    transpose_and_quantise(
-                        h, loaded[r][0], sorted_halves[r], grouped, codes, planes
-                    )
-            if 0 <= k - BEATS_TO_PASSES < BEATS:
-                for half in range(GROUP * (k - BEATS_TO_PASSES), GROUP * (k - BEATS_TO_PASSES + 1)):
-                    r_mul, h_mul = divmod(half, HALVES)
-                    if h_mul == 0:
-                        gate = out_pool.tile([P, TILES], F32)
-                        sums = out_pool.tile([P, TILES, WHOLE], F32)
-                        epilogue[r_mul] = (gate, sums)
-                    grouped, codes, planes = quantised[r_mul]
-                    products[half] = multiply(
-                        h_mul, r_mul // CHUNKS, codes, planes, epilogue[r_mul][0]
-                    )
+        for r in range(AHEAD):
+            load_x(r)
+        sort_words(0)
+        for k in range(ROUNDS + LAG + 1):
+            multiplied = k - LAG
+            emptied = multiplied - 1
+            if k + AHEAD < ROUNDS:
+                load_x(k + AHEAD)
+            if k + 1 < ROUNDS:
+                sort_words(k + 1)
+            if emptied > 0 and emptied - 1 != LAST_BEFORE_END:
+                finish(emptied - 1, slice(0, TILES))
+            if emptied >= 0:
+                for h in range(HALVES):
+                    sum_up(emptied, h)
+                    if emptied == ROUNDS - 1:
+                        finish(emptied, slice(h * HALF, (h + 1) * HALF))
+                if emptied == LAST_BEFORE_END:
+                    finish(emptied, slice(0, TILES))
+            if k < ROUNDS:
+                new_round_tiles(k)
+                for h in range(HALVES):
+                    transpose(k, h)
+                    if k > LAST_BEFORE_END - 2:
+                        quantise(k, slice(h, h + 1))
+                if k <= LAST_BEFORE_END - 2:
+                    quantise(k, slice(0, HALVES))
+            if 0 <= multiplied < ROUNDS:
+                new_epilogue_tiles(multiplied)
+                for h in range(HALVES):
+                    multiply(multiplied, h)
+                    sum_an(multiplied, h)

@@ -31,6 +31,8 @@ AHEAD = 6
 WHOLE = (F - 2) // VIEWS
 LAST_BEFORE_END = ROUNDS - LAG - 2
 LIGHT_FROM = ROUNDS - 4
+BY_GPSIMD = (ROUNDS - 3,)
+SUM_SCALE = 1.0 / (F * VIEWS)
 WEAVE = 2
 QUADRANTS = 4
 
@@ -193,7 +195,7 @@ def tile_fusion_r3d_pa_t_kernel(
             epilogue[r] = (gate, sums)
 
         def vector_sums_an(r, h):
-            return h == 1 and r % 2 == 0 and r < LIGHT_FROM - 2
+            return h == 1 and r % 4 == 0 and r < LIGHT_FROM - 2
 
         def sum_an(r, h):
             acc = products[r, h]
@@ -206,11 +208,21 @@ def tile_fusion_r3d_pa_t_kernel(
                     out=unread[:, i, :],
                     in_=acc[:, i, 1, :],
                     func=COPY,
+                    scale=1.0 if vector_sums_an(r, HALVES - 1) else SUM_SCALE,
                     accum_out=gate[:, h * HALF + i : h * HALF + i + 1],
                 )
 
-        def sum_up(r, h):
-            v, chunk = divmod(r, CHUNKS)
+        def times_gate(engine, r, rows, out, in0):
+            gate = epilogue[r][0][:, rows].unsqueeze(2).to_broadcast(list(out.shape))
+            if vector_sums_an(r, HALVES - 1):
+                engine.scalar_tensor_tensor(
+                    out=out, in0=in0, scalar=SUM_SCALE, in1=gate, op0=MULT, op1=MULT
+                )
+            else:
+                engine.tensor_tensor(out=out, in0=in0, in1=gate, op=MULT)
+
+        def add_threes(r, h):
+            v = r // CHUNKS
             acc = products[r, h]
             gate, sums = epilogue[r]
             rows = slice(h * HALF, (h + 1) * HALF)
@@ -222,36 +234,54 @@ def tile_fusion_r3d_pa_t_kernel(
                 axis=X_AXIS,
                 op=ADD,
             )
+
+        def scale_edges(r, h):
+            v, chunk = divmod(r, CHUNKS)
+            acc = products[r, h]
+            rows = slice(h * HALF, (h + 1) * HALF)
             first, last = [n for n in range(F) if not v <= n < v + VIEWS * WHOLE]
-            nc.vector.scalar_tensor_tensor(
+            times_gate(
+                nc.vector,
+                r,
+                rows,
                 out=all_edges[:, chunk, rows, 2 * v : 2 * v + 2],
                 in0=acc[:, :, 0, first : last + 1 : last - first],
-                scalar=1.0 / (F * VIEWS),
-                in1=gate[:, rows].unsqueeze(2).to_broadcast([P, HALF, 2]),
-                op0=MULT,
-                op1=MULT,
             )
 
-        def finish(r, rows):
+        def finish(r):
+            scale_sums(r, slice(0, TILES))
+            if r >= (VIEWS - 1) * CHUNKS:
+                add_border_and_store(r, slice(0, TILES))
+
+        def scale_sums(r, rows):
             v, chunk = divmod(r, CHUNKS)
-            gate, sums = epilogue[r]
+            sums = epilogue[r][1]
             result = all_results[:, chunk, rows]
-            nc.vector.scalar_tensor_tensor(
+            engine = nc.gpsimd if r in BY_GPSIMD else nc.vector
+            times_gate(
+                engine,
+                r,
+                rows,
                 out=result[:, :, (WHOLE + 1) * v : (WHOLE + 1) * v + WHOLE],
                 in0=sums[:, rows],
-                scalar=1.0 / (F * VIEWS),
-                in1=gate[:, rows].unsqueeze(2).to_broadcast([P, rows.stop - rows.start, WHOLE]),
-                op0=MULT,
-                op1=MULT,
             )
-            if v == VIEWS - 1:
+        def add_border_and_store(r, rows):
+            chunk = r % CHUNKS
+            result = all_results[:, chunk, rows]
+            border = result[:, :, WHOLE : F : WHOLE + 1]
+            edges = all_edges[:, chunk, rows]
+            if r in BY_GPSIMD:
+                terms = [edges[:, :, t : 2 * VIEWS : VIEWS] for t in range(VIEWS)]
+                nc.gpsimd.tensor_tensor(out=border, in0=terms[0], in1=terms[1], op=ADD)
+                nc.gpsimd.tensor_tensor(out=border, in0=border, in1=terms[2], op=ADD)
+            else:
                 nc.vector.tensor_reduce(
-                    out=result[:, :, WHOLE : F : WHOLE + 1],
-                    in_=all_edges[:, chunk, rows].rearrange("p i (e t) -> p i e t", t=VIEWS),
+                    out=border,
+                    in_=edges.rearrange("p i (e t) -> p i e t", t=VIEWS),
                     axis=X_AXIS,
                     op=ADD,
                 )
-                nc.sync.dma_start(out=out_chunks[chunk][:, rows], in_=result)
+            nc.sync.dma_start(out=out_chunks[chunk][:, rows], in_=result)
 
         loaded = {}
         sorted_words = {}
@@ -270,20 +300,26 @@ def tile_fusion_r3d_pa_t_kernel(
                 load_x(k + AHEAD)
             if k + 1 < ROUNDS:
                 sort_words(k + 1)
-            if emptied > 0 and emptied - 1 != LAST_BEFORE_END:
-                finish(emptied - 1, slice(0, TILES))
+            if 0 < emptied <= LAST_BEFORE_END:
+                finish(emptied - 1)
             if emptied >= 0:
                 for h in range(HALVES):
-                    sum_up(emptied, h)
-                    if emptied == ROUNDS - 1:
-                        finish(emptied, slice(h * HALF, (h + 1) * HALF))
-                if emptied == LAST_BEFORE_END:
-                    finish(emptied, slice(0, TILES))
+                    if emptied != LAST_BEFORE_END + 1:
+                        add_threes(emptied, h)
+                    if emptied == ROUNDS - 1 and h == 1:
+                        scale_sums(emptied, slice(0, HALF))
+                    scale_edges(emptied, h)
+                if emptied == ROUNDS - 1:
+                    add_border_and_store(emptied, slice(0, HALF))
+                    scale_sums(emptied, slice(HALF, TILES))
+                    add_border_and_store(emptied, slice(HALF, TILES))
+                if LAST_BEFORE_END <= emptied < ROUNDS - 1:
+                    finish(emptied)
             if k < ROUNDS:
                 new_round_tiles(k)
                 for h in range(HALVES):
                     transpose(k, h)
-                    if k > LAST_BEFORE_END - 2:
+                    if k > LAST_BEFORE_END - 2 and (k, h) != (ROUNDS - 1, 1):
                         quantise(k, slice(h, h + 1))
                 if k <= LAST_BEFORE_END - 2:
                     quantise(k, slice(0, HALVES))
@@ -291,4 +327,11 @@ def tile_fusion_r3d_pa_t_kernel(
                 new_epilogue_tiles(multiplied)
                 for h in range(HALVES):
                     multiply(multiplied, h)
-                    sum_an(multiplied, h)
+                    if k != ROUNDS - 1:
+                        sum_an(multiplied, h)
+                if k == ROUNDS - 1:
+                    for h in range(HALVES):
+                        add_threes(multiplied, h)
+                    quantise(k, slice(1, 2))
+                    for h in range(HALVES):
+                        sum_an(multiplied, h)

from contextlib import ExitStack

import concourse.mybir as mybir
from concourse.masks import make_identity

F32 = mybir.dt.float32
BF16 = mybir.dt.bfloat16
I32 = mybir.dt.int32
U32 = mybir.dt.uint32
U8 = mybir.dt.uint8
FP8X4 = mybir.dt.float8_e4m3fn_x4
ADD = mybir.AluOpType.add
MULT = mybir.AluOpType.mult
X_AXIS = mybir.AxisListType.X
COPY = mybir.ActivationFunctionType.Copy

P = 128
PACK = 4
K_PASS = P * PACK
B, DIN, F, VIEWS = 4096, 1024, 128, 3
PASSES = DIN // K_PASS
PAIRS = PACK // 2
PASS_WORDS = K_PASS // 2
HALF = 2
HALVES = 2
TILES = HALF * HALVES
CHUNKS = B // (P * TILES)
ROUNDS = CHUNKS * VIEWS
LAG = 2
AHEAD = 6
WHOLE = (F - 2) // VIEWS
LAST_BEFORE_END = ROUNDS - LAG - 2
LIGHT_FROM = ROUNDS - 4
BY_GPSIMD = (ROUNDS - 3,)
SUM_SCALE = 1.0 / (F * VIEWS)
WEAVE = 2
QUADRANTS = 4

FLOPS = 2 * 2 * VIEWS * B * DIN * F


def sorted_tiles(r):
    return 3 if r % 2 == 1 and LAG < r < LIGHT_FROM else 2


def tile_fusion_r3d_pa_t_kernel(
    tc,
    x_dash, x_rear, x_right,
    Wd_nm_words, Wd_nm_scales, Wd_an_words, Wd_an_scales,
    Wr_nm_words, Wr_nm_scales, Wr_an_words, Wr_an_scales,
    Wt_nm_words, Wt_nm_scales, Wt_an_words, Wt_an_scales,
    out,
):
    nc = tc.nc
    x_chunks = [
        x.rearrange("(c p i) k -> c p i k", p=P, i=TILES)
        for x in (x_dash, x_rear, x_right)
    ]
    out_chunks = out.rearrange("(c p i) n -> c p i n", p=P, i=TILES)
    weights = [
        ((Wd_nm_words, Wd_nm_scales), (Wd_an_words, Wd_an_scales)),
        ((Wr_nm_words, Wr_nm_scales), (Wr_an_words, Wr_an_scales)),
        ((Wt_nm_words, Wt_nm_scales), (Wt_an_words, Wt_an_scales)),
    ]

    with ExitStack() as ctx:
        consts = ctx.enter_context(tc.tile_pool(name="consts", bufs=1))
        x_pool = ctx.enter_context(tc.tile_pool(name="x_pool", bufs=AHEAD + 2))
        mx_pool = ctx.enter_context(tc.tile_pool(name="mx_pool", bufs=LAG + 2))
        out_pool = ctx.enter_context(tc.tile_pool(name="out_pool", bufs=3))
        t_psum = ctx.enter_context(tc.psum_pool(name="t_psum", bufs=TILES))
        acc_psum = ctx.enter_context(tc.psum_pool(name="acc_psum", bufs=2 * HALVES))
        ctx.enter_context(tc.manual_schedule())

        ident = consts.tile([P, P], F32)
        make_identity(nc, ident[:])
        table_warmer = consts.tile([P, 1], F32)
        nc.scalar.activation(out=table_warmer[:], in_=ident[:, 0:1], func=COPY)
        w_words = consts.tile([P, VIEWS, PASSES, 2 * F], U32, align_bytes=64)
        w_planes = consts.tile([P, VIEWS, PASSES, 2 * F], U8, align_bytes=64)
        nc.vector.memset(w_planes[:].rearrange("p v g n -> p (v g n)").bitcast(I32), 0)

        def load_weight_piece(v, s, quad):
            words, scales = weights[v][s]
            cols = slice(s * F, (s + 1) * F)
            if quad < 0:
                nc.sync.dma_start(
                    out=w_words[:, v, :, cols].bitcast(I32),
                    in_=words.rearrange("g p n t -> p g (n t)").bitcast(I32),
                )
            else:
                nc.sync.dma_start(
                    out=w_planes[32 * quad : 32 * quad + 4, v, :, cols].bitcast(I32),
                    in_=scales[:, 4 * quad : 4 * quad + 4, :]
                    .rearrange("g r n -> r g n")
                    .bitcast(I32),
                )

        pieces = [
            (v, s, quad) for v in range(VIEWS) for s in range(2) for quad in range(-1, QUADRANTS)
        ]
        queued = {"pieces": 0}

        def weave_weights(views_wanted):
            upto = min(queued["pieces"] + WEAVE, views_wanted * len(pieces) // VIEWS)
            for piece in pieces[queued["pieces"] : upto]:
                load_weight_piece(*piece)
            queued["pieces"] = max(queued["pieces"], upto)

        def load_x(r):
            v, chunk = divmod(r, CHUNKS)
            x_round = x_pool.tile([P, TILES, DIN], BF16)
            for h in range(HALVES):
                step = 1 if r == 0 else HALF
                for i in range(h * HALF, (h + 1) * HALF, step):
                    nc.sync.dma_start(
                        out=x_round[:, i : i + step], in_=x_chunks[v][chunk, :, i : i + step]
                    )
                weave_weights(1 if r < AHEAD else VIEWS)
            loaded[r] = x_round

        def sort_words(r):
            count = sorted_tiles(r)
            x_sorted = mx_pool.tile([P, PASSES, count, PAIRS, P], F32, name="x_sorted")
            step = 1 if r == 0 else count
            for i in range(0, count, step):
                first = TILES - count + i
                nc.vector.tensor_copy(
                    out=x_sorted[:, :, i : i + step],
                    in_=loaded[r][:, first : first + step]
                    .bitcast(F32)
                    .rearrange("p i (g c u) -> p g i u c", g=PASSES, u=PAIRS),
                )
            sorted_words[r] = x_sorted

        def new_round_tiles(r):
            grouped = mx_pool.tile([P, HALVES, HALF, PASSES, P, PACK], BF16, align_bytes=64)
            codes = mx_pool.tile([P, HALVES, HALF, PASSES, P], U32, align_bytes=64)
            planes = mx_pool.tile([P, HALVES, HALF, PASSES, P], U8, align_bytes=64)
            quantised[r] = (grouped, codes, planes)

        def transpose(r, h):
            grouped = quantised[r][0]
            direct_words = loaded[r][:].bitcast(F32)
            first_sorted = TILES - sorted_tiles(r)
            grouped_words = grouped[:].bitcast(F32)
            for i in range(HALF):
                xt = t_psum.tile([P, PASSES, PAIRS, P], F32)
                for g in range(PASSES):
                    for u in range(PAIRS):
                        tile = h * HALF + i
                        if tile < first_sorted:
                            words = direct_words[
                                :, tile, g * PASS_WORDS + u : (g + 1) * PASS_WORDS : PAIRS
                            ]
                        else:
                            words = sorted_words[r][:, g, tile - first_sorted, u, :]
                        nc.tensor.transpose(xt[:, g, u, :], words, ident[:])
                nc.scalar.copy(
                    out=grouped_words[:, h, i], in_=xt[:].rearrange("p g u b -> p g b u")
                )

        def quantise(r, halves):
            grouped, codes, planes = quantised[r]
            nc.vector.quantize_mx(
                out=codes[:, halves].rearrange("p h i g b -> p (h i g b)").bitcast(FP8X4),
                scales=planes[:, halves].rearrange("p h i g b -> p (h i g b)"),
                in_=grouped[:, halves].rearrange("p h i g b t -> p (h i g b t)"),
            )

        def multiply(r, h):
            codes, planes = quantised[r][1:]
            v = r // CHUNKS
            if r == ROUNDS - 1:
                xt = t_psum.tile([P, PASSES, PAIRS, P], F32)
                acc = xt
            else:
                acc = acc_psum.tile([P, HALF, 2, F], F32)
            for i in range(HALF):
                for g in range(PASSES):
                    nc.tensor.matmul_mx(
                        out=acc[:, i].rearrange("p s n -> p (s n)"),
                        lhsT=codes[:, h, i, g, :].bitcast(FP8X4),
                        lhsT_scale=planes[:, h, i, g, :],
                        rhs=w_words[:, v, g, :].bitcast(FP8X4),
                        rhs_scale=w_planes[:, v, g, :],
                        start=(g == 0),
                        stop=(g == PASSES - 1),
                    )
            products[r, h] = acc

        def new_epilogue_tiles(r):
            gate = out_pool.tile([P, TILES], F32)
            sums = out_pool.tile([P, TILES, WHOLE], F32)
            epilogue[r] = (gate, sums)

        def vector_sums_an(r, h):
            return h == 1 and r % 4 == 0 and r < LIGHT_FROM - 2

        def sum_an(r, h):
            acc = products[r, h]
            gate = epilogue[r][0]
            if vector_sums_an(r, h):
                return
            unread = out_pool.tile([P, HALF, F], F32, name="unread%d" % h)
            for i in range(HALF):
                nc.scalar.activation(
                    out=unread[:, i, :],
                    in_=acc[:, i, 1, :],
                    func=COPY,
                    scale=1.0 if vector_sums_an(r, HALVES - 1) else SUM_SCALE,
                    accum_out=gate[:, h * HALF + i : h * HALF + i + 1],
                )

        def times_gate(engine, r, rows, out, in0):
            gate = epilogue[r][0][:, rows].unsqueeze(2).to_broadcast(list(out.shape))
            if vector_sums_an(r, HALVES - 1):
                engine.scalar_tensor_tensor(
                    out=out, in0=in0, scalar=SUM_SCALE, in1=gate, op0=MULT, op1=MULT
                )
            else:
                engine.tensor_tensor(out=out, in0=in0, in1=gate, op=MULT)

        def add_threes(r, h):
            v = r // CHUNKS
            acc = products[r, h]
            gate, sums = epilogue[r]
            rows = slice(h * HALF, (h + 1) * HALF)
            if vector_sums_an(r, h):
                nc.vector.tensor_reduce(out=gate[:, rows], in_=acc[:, :, 1, :], axis=X_AXIS, op=ADD)
            nc.vector.tensor_reduce(
                out=sums[:, rows, :],
                in_=acc[:, :, 0, v : v + VIEWS * WHOLE].rearrange("p i (m t) -> p i m t", t=VIEWS),
                axis=X_AXIS,
                op=ADD,
            )

        def scale_edges(r, h):
            v, chunk = divmod(r, CHUNKS)
            acc = products[r, h]
            rows = slice(h * HALF, (h + 1) * HALF)
            first, last = [n for n in range(F) if not v <= n < v + VIEWS * WHOLE]
            times_gate(
                nc.vector,
                r,
                rows,
                out=all_edges[:, chunk, rows, 2 * v : 2 * v + 2],
                in0=acc[:, :, 0, first : last + 1 : last - first],
            )

        def finish(r):
            scale_sums(r, slice(0, TILES))
            if r >= (VIEWS - 1) * CHUNKS:
                add_border_and_store(r, slice(0, TILES))

        def scale_sums(r, rows):
            v, chunk = divmod(r, CHUNKS)
            sums = epilogue[r][1]
            result = all_results[:, chunk, rows]
            engine = nc.gpsimd if r in BY_GPSIMD else nc.vector
            times_gate(
                engine,
                r,
                rows,
                out=result[:, :, (WHOLE + 1) * v : (WHOLE + 1) * v + WHOLE],
                in0=sums[:, rows],
            )
        def add_border_and_store(r, rows):
            chunk = r % CHUNKS
            result = all_results[:, chunk, rows]
            border = result[:, :, WHOLE : F : WHOLE + 1]
            edges = all_edges[:, chunk, rows]
            if r in BY_GPSIMD:
                terms = [edges[:, :, t : 2 * VIEWS : VIEWS] for t in range(VIEWS)]
                nc.gpsimd.tensor_tensor(out=border, in0=terms[0], in1=terms[1], op=ADD)
                nc.gpsimd.tensor_tensor(out=border, in0=border, in1=terms[2], op=ADD)
            else:
                nc.vector.tensor_reduce(
                    out=border,
                    in_=edges.rearrange("p i (e t) -> p i e t", t=VIEWS),
                    axis=X_AXIS,
                    op=ADD,
                )
            nc.sync.dma_start(out=out_chunks[chunk][:, rows], in_=result)

        loaded = {}
        sorted_words = {}
        quantised = {}
        products = {}
        epilogue = {}
        all_edges = consts.tile([P, CHUNKS, TILES, 2 * VIEWS], F32)
        all_results = consts.tile([P, CHUNKS, TILES, F], F32)
        for r in range(AHEAD):
            load_x(r)
        sort_words(0)
        for k in range(ROUNDS + LAG + 1):
            multiplied = k - LAG
            emptied = multiplied - 1
            if k + AHEAD < ROUNDS:
                load_x(k + AHEAD)
            if k + 1 < ROUNDS:
                sort_words(k + 1)
            if 0 < emptied <= LAST_BEFORE_END:
                finish(emptied - 1)
            if emptied >= 0:
                for h in range(HALVES):
                    if emptied != LAST_BEFORE_END + 1:
                        add_threes(emptied, h)
                    if emptied == ROUNDS - 1 and h == 1:
                        scale_sums(emptied, slice(0, HALF))
                    scale_edges(emptied, h)
                if emptied == ROUNDS - 1:
                    add_border_and_store(emptied, slice(0, HALF))
                    scale_sums(emptied, slice(HALF, TILES))
                    add_border_and_store(emptied, slice(HALF, TILES))
                if LAST_BEFORE_END <= emptied < ROUNDS - 1:
                    finish(emptied)
            if k < ROUNDS:
                new_round_tiles(k)
                for h in range(HALVES):
                    transpose(k, h)
                    if k > LAST_BEFORE_END - 2 and (k, h) != (ROUNDS - 1, 1):
                        quantise(k, slice(h, h + 1))
                if k <= LAST_BEFORE_END - 2:
                    quantise(k, slice(0, HALVES))
            if 0 <= multiplied < ROUNDS:
                new_epilogue_tiles(multiplied)
                for h in range(HALVES):
                    multiply(multiplied, h)
                    if k != ROUNDS - 1:
                        sum_an(multiplied, h)
                if k == ROUNDS - 1:
                    for h in range(HALVES):
                        add_threes(multiplied, h)
                    quantise(k, slice(1, 2))
                    for h in range(HALVES):
                        sum_an(multiplied, h)
